import numpy as np
import ml_dtypes


def mxq(x, axis, fmt="e4m3"):
    dtype, down = {"e4m3": (ml_dtypes.float8_e4m3fn, 7), "e5m2": (ml_dtypes.float8_e5m2, 14)}[fmt]
    v = np.moveaxis(np.asarray(x, np.float32).astype(ml_dtypes.bfloat16).astype(np.float64), axis, -1)
    blocks = v.reshape(v.shape[:-1] + (-1, 32))
    amax = np.abs(blocks).max(-1, keepdims=True)
    byte = np.maximum(np.where(amax > 0, np.frexp(amax)[1] - 1 + 127, 0) - down, 1)
    scale = np.exp2(byte - 127.0)
    codes = (blocks / scale).astype(np.float32).astype(dtype).astype(np.float64)
    return np.moveaxis((codes * scale).reshape(v.shape), -1, axis)


WIDE = False


def mx_kscale(k):
    if not WIDE:
        return np.ones(k)
    levels = np.array([10, -10, 5, -5, 0])
    a = np.random.permutation(np.resize(levels, k // 512 * 4)).reshape(k // 512, 4)
    idx = np.arange(k)
    return np.exp2(a[idx // 512, idx % 128 // 32])


BF16 = ml_dtypes.bfloat16


def bf(x):
    return np.asarray(x, np.float32).astype(BF16)


def f64(x):
    return np.asarray(x).astype(np.float64)


B, NT, N, C, DV, TM = 2, 128, 512, 1024, 1024, 128


def softmax(s):
    e = np.exp(s - s.max(-1, keepdims=True))
    return e / e.sum(-1, keepdims=True)


def setup_inputs():
    s = mx_kscale(C)
    q = np.random.standard_normal((B, 1, C)) + np.random.standard_normal((B, NT, C))
    k = bf(np.random.standard_normal((B, N, C)) * 1.4)
    ki = bf(np.random.standard_normal((B, N, C)) * 1.4)
    ki[-1] = k[-1]
    return {'q': bf(q), 'k': k, 'ki': ki,
            'xs': bf(np.random.standard_normal((B, N, C)) * s),
            'xis': bf(np.random.standard_normal((B, N, C)) * s),
            'Wv': bf(np.random.standard_normal((C, DV)) * 1.8 / np.sqrt(C) / s[:, None])}


def reference(q, k, ki, xs, xis, Wv):
    scale = C ** -0.5
    aw = softmax(f64(q) @ f64(k).transpose(0, 2, 1) * scale)
    awi = softmax(f64(q) @ f64(ki).transpose(0, 2, 1) * scale)
    D = aw - awi
    ones_cnt = np.where(D > 0, 1.0, 0.0).sum(axis=1)
    half_cnt = np.where(D == 0, 1.0, 0.0).sum(axis=1)
    rgb_ratio = (ones_cnt / NT)[..., None]
    eq_ratio = (half_cnt / NT)[..., None]
    tir_ratio = 1.0 - rgb_ratio - eq_ratio
    wv = mxq(f64(Wv), 0, 'e4m3')
    v = mxq(f64(xs), 2, 'e4m3') @ wv
    vi = mxq(f64(xis), 2, 'e4m3') @ wv
    return v * (rgb_ratio + eq_ratio) + vi * (tir_ratio + eq_ratio)

@@ -1,0 +1,264 @@
+from contextlib import ExitStack
+
+import concourse.mybir as mybir
+from concourse.masks import make_identity
+
+BF16 = mybir.dt.bfloat16
+F32 = mybir.dt.float32
+U32 = mybir.dt.uint32
+U8 = mybir.dt.uint8
+FP8X4 = mybir.dt.float8_e4m3fn_x4
+ALU = mybir.AluOpType
+ACT = mybir.ActivationFunctionType
+AXIS = mybir.AxisListType
+
+P = 128
+BATCH = 2
+QUERIES = 128
+KEYS = 512
+C = 1024
+DV = 1024
+KEY_TILES = KEYS // P
+PAIR = 2
+WORD_CHUNKS = C // PAIR // P
+PACK = 4
+PASSES = C // (P * PACK)
+BANK = 512
+DV_HALVES = DV // BANK
+COUNT_COLS = 32
+SCALE = C**-0.5
+
+FLOPS = 2 * BATCH * 2 * QUERIES * KEYS * C + 2 * BATCH * 2 * KEYS * C * DV
+
+
+def tile_crossattention_for_fusion_temporal_pa_kernel(tc, q, k, ki, xs, xis, Wv, out):
+    nc = tc.nc
+    with ExitStack() as ctx:
+        resident = ctx.enter_context(tc.tile_pool(name="resident", bufs=1))
+        rotating = ctx.enter_context(tc.tile_pool(name="rotating", bufs=2))
+        small = ctx.enter_context(tc.tile_pool(name="small", bufs=4))
+        psum = ctx.enter_context(tc.psum_pool(name="psum", bufs=8))
+
+        def load_queries(b):
+            rows_sb = resident.tile([P, C], BF16, name="q_sb%d" % b)
+            nc.sync.dma_start(out=rows_sb[:], in_=q[b])
+            return rows_sb
+
+        def load_rows(name, rows):
+            rows_sb = resident.tile([P, KEY_TILES * C], BF16, name=name)
+            nc.sync.dma_start(out=rows_sb[:], in_=rows.rearrange("(p j) c -> p (j c)", j=KEY_TILES))
+            return rows_sb
+
+        def load_weights():
+            w_raw = resident.tile([P, PASSES * PACK * DV], BF16, name="w_raw")
+            halves_view = w_raw[:].rearrange("p (g u e d) -> p g u e d", g=PASSES, u=2, e=PAIR)
+            for g in range(PASSES):
+                rows = Wv[g * P * PACK : (g + 1) * P * PACK, :]
+                nc.sync.dma_start(
+                    out=halves_view[:, g], in_=rows.rearrange("(u p e) d -> p u e d", u=2, e=PAIR)
+                )
+            return w_raw
+
+        queries_sb = [None] * BATCH
+        keys_sb = [None] * BATCH
+        queries_sb[0] = load_queries(0)
+        keys_sb[0] = (load_rows("k_sb0", k[0]), load_rows("ki_sb0", ki[0]))
+        w_raw = load_weights()
+        queries_sb[1] = load_queries(1)
+        keys_sb[1] = (load_rows("k_sb1", k[1]), load_rows("ki_sb1", ki[1]))
+        tokens_sb = [
+            load_rows("x_sb%d%d" % (b, stream), rows[b])
+            for b in range(BATCH)
+            for stream, rows in enumerate((xs, xis))
+        ]
+
+        ident = resident.tile([P, P], F32, name="ident")
+        make_identity(nc, ident[:])
+        vote_share = resident.tile([P, COUNT_COLS], BF16, name="vote_share")
+        nc.vector.memset(vote_share[:], 1.0 / QUERIES)
+
+        def transpose_words(bank_cols, words):
+            nc.tensor.transpose(bank_cols, words, ident[:])
+
+        def mix_factors(b):
+            q_words = queries_sb[b][:].bitcast(F32)
+            q_bank = psum.tile([P, BANK], F32, tag="bank")
+            for g in range(WORD_CHUNKS):
+                transpose_words(q_bank[:, g * P : (g + 1) * P], q_words[:, g * P : (g + 1) * P])
+            qT = rotating.tile([P, PAIR * BANK], BF16, tag="qT")
+            nc.vector.tensor_copy(out=qT[:], in_=q_bank[:].bitcast(BF16))
+            qT_view = qT[:].rearrange("p (g r e) -> p g r e", g=WORD_CHUNKS, e=PAIR)
+
+            attention = []
+            for rows_sb in keys_sb[b]:
+                key_words = rows_sb[:].bitcast(F32).rearrange("p (j w) -> p j w", j=KEY_TILES)
+                kT = rotating.tile([P, WORD_CHUNKS * PAIR * BANK], BF16, tag="kT")
+                for g in range(WORD_CHUNKS):
+                    k_bank = psum.tile([P, BANK], F32, tag="bank")
+                    for j in range(KEY_TILES):
+                        transpose_words(
+                            k_bank[:, j * P : (j + 1) * P], key_words[:, j, g * P : (g + 1) * P]
+                        )
+                    piece = kT[:, g * PAIR * BANK : (g + 1) * PAIR * BANK]
+                    if g % 2 == 0:
+                        nc.scalar.copy(out=piece, in_=k_bank[:].bitcast(BF16))
+                    else:
+                        nc.vector.tensor_copy(out=piece, in_=k_bank[:].bitcast(BF16))
+                kT_view = kT[:].rearrange("p (g n e) -> p g n e", g=WORD_CHUNKS, e=PAIR)
+
+                score = psum.tile([P, KEYS], F32, tag="bank")
+                for g in range(WORD_CHUNKS):
+                    for e in range(PAIR):
+                        nc.tensor.matmul(
+                            score[:],
+                            lhsT=qT_view[:, g, :, e],
+                            rhs=kT_view[:, g, :, e],
+                            start=(g == 0 and e == 0),
+                            stop=(g == WORD_CHUNKS - 1 and e == PAIR - 1),
+                        )
+
+                top = small.tile([P, 1], F32, tag="top")
+                nc.vector.reduce_max(out=top[:], in_=score[:], axis=AXIS.X)
+                shift = small.tile([P, 1], F32, tag="shift")
+                nc.vector.tensor_scalar_mul(out=shift[:], in0=top[:], scalar1=-SCALE)
+                attn = rotating.tile([P, KEYS], F32, tag="attn", bufs=4)
+                total = small.tile([P, 1], F32, tag="total")
+                nc.scalar.activation(
+                    out=attn[:],
+                    in_=score[:],
+                    func=ACT.Exp,
+                    bias=shift[:],
+                    scale=SCALE,
+                    accum_out=total[:],
+                )
+                inverse = small.tile([P, 1], F32, tag="inverse")
+                nc.vector.reciprocal(out=inverse[:], in_=total[:])
+                nc.vector.tensor_scalar_mul(out=attn[:], in0=attn[:], scalar1=inverse[:])
+                attention.append(attn)
+
+            not_less = rotating.tile([P, KEYS], BF16, tag="not_less")
+            nc.vector.tensor_tensor(
+                out=not_less[:], in0=attention[0][:], in1=attention[1][:], op=ALU.is_ge
+            )
+            not_more = rotating.tile([P, KEYS], BF16, tag="not_more")
+            nc.vector.tensor_tensor(
+                out=not_more[:], in0=attention[0][:], in1=attention[1][:], op=ALU.is_le
+            )
+
+            counts = psum.tile([P, KEY_TILES * 2 * COUNT_COLS], F32, tag="bank")
+            for j in range(KEY_TILES):
+                for side, votes in enumerate((not_less, not_more)):
+                    first = (2 * j + side) * COUNT_COLS
+                    nc.tensor.matmul(
+                        counts[:, first : first + COUNT_COLS],
+                        lhsT=votes[:, j * P : (j + 1) * P],
+                        rhs=vote_share[:],
+                        start=True,
+                        stop=True,
+                    )
+            factors = resident.tile([P, KEY_TILES * 2], F32, name="factors%d" % b)
+            nc.vector.tensor_copy(
+                out=factors[:], in_=counts[:].rearrange("p (i n) -> p i n", n=COUNT_COLS)[:, :, 0]
+            )
+            return factors
+
+        w_grouped = resident.tile([P, PASSES * DV * PACK], BF16, name="w_grouped", align_bytes=64)
+        w_codes = resident.tile([P, PASSES * DV], U32, name="w_codes", align_bytes=64)
+        w_scales = resident.tile([P, PASSES * DV], U8, name="w_scales", align_bytes=64)
+
+        def quantise_weights():
+            raw_view = w_raw[:].rearrange("p (g t d) -> p g t d", g=PASSES, t=PACK)
+            grouped_view = w_grouped[:].rearrange("p (g d t) -> p g d t", g=PASSES, t=PACK)
+            for h in range(DV_HALVES):
+                cols = slice(h * BANK, (h + 1) * BANK)
+                for g in range(PASSES):
+                    nc.vector.tensor_copy(
+                        out=grouped_view[:, g, cols, :].rearrange("p (c i) t -> p c t i", i=4),
+                        in_=raw_view[:, g, :, cols].rearrange("p t (c i) -> p c t i", i=4),
+                    )
+                for g in range(PASSES):
+                    first = g * DV + h * BANK
+                    nc.vector.quantize_mx(
+                        out=w_codes[:, first : first + BANK].bitcast(FP8X4),
+                        scales=w_scales[:, first : first + BANK],
+                        in_=w_grouped[:, PACK * first : PACK * (first + BANK)],
+                    )
+
+        def quantise_tokens(rows_sb):
+            x_words = rows_sb[:].bitcast(F32).rearrange("p (j w) -> p j w", j=KEY_TILES)
+            grouped = rotating.tile([P, PASSES * KEYS * PACK], BF16, tag="x_grouped", align_bytes=64)
+            grouped_words = grouped[:].bitcast(F32).rearrange("p (g n u) -> p g n u", g=PASSES, u=2)
+            codes = rotating.tile([P, PASSES * KEYS], U32, tag="x_codes", align_bytes=64)
+            scales = rotating.tile([P, PASSES * KEYS], U8, tag="x_scales", align_bytes=64)
+            for g in range(PASSES):
+                for half in range(KEY_TILES // 2):
+                    x_bank = psum.tile([P, BANK], F32, tag="bank")
+                    bank_view = x_bank[:].rearrange("p (u n) -> p u n", u=2)
+                    for u in range(2):
+                        for i in range(2):
+                            first_word = (2 * g + u) * P
+                            transpose_words(
+                                bank_view[:, u, i * P : (i + 1) * P],
+                                x_words[:, 2 * half + i, first_word : first_word + P],
+                            )
+                    nc.scalar.copy(
+                        out=grouped_words[:, g, half * 2 * P : (half + 1) * 2 * P, :],
+                        in_=x_bank[:].rearrange("p (u n) -> p n u", u=2),
+                    )
+            for g in range(PASSES):
+                nc.vector.quantize_mx(
+                    out=codes[:, g * KEYS : (g + 1) * KEYS].bitcast(FP8X4),
+                    scales=scales[:, g * KEYS : (g + 1) * KEYS],
+                    in_=grouped[:, g * KEYS * PACK : (g + 1) * KEYS * PACK],
+                )
+            return codes, scales
+
+        def project(b, stream, codes, scales, factors, scaled_v):
+            out_view = out[b].rearrange("(p j) d -> p j d", j=KEY_TILES)
+            for j in range(KEY_TILES):
+                if stream == 1:
+                    mixed = rotating.tile([P, DV], F32, tag="mixed", bufs=3)
+                for h in range(DV_HALVES):
+                    acc = psum.tile([P, BANK], F32, tag="bank")
+                    for g in range(PASSES):
+                        tokens = slice(g * KEYS + j * P, g * KEYS + (j + 1) * P)
+                        cols = slice(g * DV + h * BANK, g * DV + (h + 1) * BANK)
+                        nc.tensor.matmul_mx(
+                            out=acc[:],
+                            lhsT=codes[:, tokens].bitcast(FP8X4),
+                            lhsT_scale=scales[:, tokens],
+                            rhs=w_codes[:, cols].bitcast(FP8X4),
+                            rhs_scale=w_scales[:, cols],
+                            start=(g == 0),
+                            stop=(g == PASSES - 1),
+                        )
+                    kept = scaled_v[:, j * DV + h * BANK : j * DV + (h + 1) * BANK]
+                    if stream == 0:
+                        nc.scalar.activation(
+                            out=kept, in_=acc[:], func=ACT.Copy, scale=factors[:, 2 * j : 2 * j + 1]
+                        )
+                    else:
+                        nc.vector.scalar_tensor_tensor(
+                            out=mixed[:, h * BANK : (h + 1) * BANK],
+                            in0=acc[:],
+                            scalar=factors[:, 2 * j + 1 : 2 * j + 2],
+                            in1=kept,
+                            op0=ALU.mult,
+                            op1=ALU.add,
+                        )
+                if stream == 1:
+                    nc.sync.dma_start(out=out_view[:, j, :], in_=mixed[:])
+
+        factors_of = [None] * BATCH
+        factors_of[0] = mix_factors(0)
+        quantise_weights()
+        factors_of[1] = mix_factors(1)
+        ready = quantise_tokens(tokens_sb[0])
+        for b in range(BATCH):
+            scaled_v = rotating.tile([P, KEY_TILES * DV], F32, tag="scaled_v")
+            for stream in range(2):
+                codes, scales = ready
+                following = 2 * b + stream + 1
+                if following < len(tokens_sb):
+                    ready = quantise_tokens(tokens_sb[following])
+                project(b, stream, codes, scales, factors_of[b], scaled_v)

@@ -26,6 +26,8 @@ PASSES = C // (P * PACK)
 BANK = 512
 DV_HALVES = DV // BANK
 COUNT_COLS = 32
+UNIT_BANKS = 4
+SHARED_VECTOR_BANKS = 1
 SCALE = C**-0.5
 
 FLOPS = 2 * BATCH * 2 * QUERIES * KEYS * C + 2 * BATCH * 2 * KEYS * C * DV
@@ -38,36 +40,33 @@ def tile_crossattention_for_fusion_temporal_pa_kernel(tc, q, k, ki, xs, xis, Wv,
         rotating = ctx.enter_context(tc.tile_pool(name="rotating", bufs=2))
         small = ctx.enter_context(tc.tile_pool(name="small", bufs=4))
         psum = ctx.enter_context(tc.psum_pool(name="psum", bufs=8))
+        ctx.enter_context(tc.manual_schedule())
 
-        def load_queries(b):
-            rows_sb = resident.tile([P, C], BF16, name="q_sb%d" % b)
-            nc.sync.dma_start(out=rows_sb[:], in_=q[b])
-            return rows_sb
+        w_raw = resident.tile([P, PASSES * PACK * DV], BF16, name="w_raw")
+        halves_view = w_raw[:].rearrange("p (g u e d) -> p g u e d", g=PASSES, u=2, e=PAIR)
+        for g in range(PASSES):
+            rows = Wv[g * P * PACK : (g + 1) * P * PACK, :]
+            nc.sync.dma_start(
+                out=halves_view[:, g], in_=rows.rearrange("(u p e) d -> p u e d", u=2, e=PAIR)
+            )
+
+        q_sb = resident.tile([P, BATCH * C], BF16, name="q_sb")
+        nc.sync.dma_start(
+            out=q_sb[:].rearrange("p (b c) -> p b c", b=BATCH), in_=q.rearrange("b r c -> r b c")
+        )
 
         def load_rows(name, rows):
             rows_sb = resident.tile([P, KEY_TILES * C], BF16, name=name)
             nc.sync.dma_start(out=rows_sb[:], in_=rows.rearrange("(p j) c -> p (j c)", j=KEY_TILES))
             return rows_sb
 
-        def load_weights():
-            w_raw = resident.tile([P, PASSES * PACK * DV], BF16, name="w_raw")
-            halves_view = w_raw[:].rearrange("p (g u e d) -> p g u e d", g=PASSES, u=2, e=PAIR)
-            for g in range(PASSES):
-                rows = Wv[g * P * PACK : (g + 1) * P * PACK, :]
-                nc.sync.dma_start(
-                    out=halves_view[:, g], in_=rows.rearrange("(u p e) d -> p u e d", u=2, e=PAIR)
-                )
-            return w_raw
-
-        queries_sb = [None] * BATCH
-        keys_sb = [None] * BATCH
-        queries_sb[0] = load_queries(0)
-        keys_sb[0] = (load_rows("k_sb0", k[0]), load_rows("ki_sb0", ki[0]))
-        w_raw = load_weights()
-        queries_sb[1] = load_queries(1)
-        keys_sb[1] = (load_rows("k_sb1", k[1]), load_rows("ki_sb1", ki[1]))
+        keys_sb = [
+            load_rows("keys_sb%d%d" % (b, stream), rows[b])
+            for b in range(BATCH)
+            for stream, rows in enumerate((k, ki))
+        ]
         tokens_sb = [
-            load_rows("x_sb%d%d" % (b, stream), rows[b])
+            load_rows("tokens_sb%d%d" % (b, stream), rows[b])
             for b in range(BATCH)
             for stream, rows in enumerate((xs, xis))
         ]
@@ -76,78 +75,139 @@ def tile_crossattention_for_fusion_temporal_pa_kernel(tc, q, k, ki, xs, xis, Wv,
         make_identity(nc, ident[:])
         vote_share = resident.tile([P, COUNT_COLS], BF16, name="vote_share")
         nc.vector.memset(vote_share[:], 1.0 / QUERIES)
+        zero = small.tile([P, 1], F32, tag="zero")
+        nc.vector.memset(zero[:], 0.0)
+        one = small.tile([P, 1], F32, tag="one")
+        nc.scalar.activation(out=one[:], in_=zero[:], func=ACT.Exp)
+
+        w_grouped = resident.tile([P, PASSES * DV * PACK], BF16, name="w_grouped", align_bytes=64)
+        w_codes = resident.tile([P, PASSES * DV], U32, name="w_codes", align_bytes=64)
+        w_scales = resident.tile([P, PASSES * DV], U8, name="w_scales", align_bytes=64)
+        raw_view = w_raw[:].rearrange("p (g t d) -> p g t d", g=PASSES, t=PACK)
+        grouped_view = w_grouped[:].rearrange("p (g d t) -> p g d t", g=PASSES, t=PACK)
+        for g in range(PASSES):
+            for h in range(DV_HALVES):
+                cols = slice(h * BANK, (h + 1) * BANK)
+                nc.vector.tensor_copy(
+                    out=grouped_view[:, g, cols, :].rearrange("p (c i) t -> p c t i", i=4),
+                    in_=raw_view[:, g, :, cols].rearrange("p t (c i) -> p c t i", i=4),
+                )
+        for g in range(PASSES):
+            nc.vector.quantize_mx(
+                out=w_codes[:, g * DV : (g + 1) * DV].bitcast(FP8X4),
+                scales=w_scales[:, g * DV : (g + 1) * DV],
+                in_=w_grouped[:, g * DV * PACK : (g + 1) * DV * PACK],
+            )
 
         def transpose_words(bank_cols, words):
             nc.tensor.transpose(bank_cols, words, ident[:])
 
-        def mix_factors(b):
-            q_words = queries_sb[b][:].bitcast(F32)
+        qT = resident.tile([P, BATCH * PAIR * BANK], BF16, name="qT")
+        q_words = q_sb[:].bitcast(F32)
+        for b in range(BATCH):
             q_bank = psum.tile([P, BANK], F32, tag="bank")
             for g in range(WORD_CHUNKS):
-                transpose_words(q_bank[:, g * P : (g + 1) * P], q_words[:, g * P : (g + 1) * P])
-            qT = rotating.tile([P, PAIR * BANK], BF16, tag="qT")
-            nc.vector.tensor_copy(out=qT[:], in_=q_bank[:].bitcast(BF16))
-            qT_view = qT[:].rearrange("p (g r e) -> p g r e", g=WORD_CHUNKS, e=PAIR)
+                first = (b * WORD_CHUNKS + g) * P
+                transpose_words(q_bank[:, g * P : (g + 1) * P], q_words[:, first : first + P])
+            nc.scalar.copy(
+                out=qT[:, b * PAIR * BANK : (b + 1) * PAIR * BANK], in_=q_bank[:].bitcast(BF16)
+            )
+        qT_view = qT[:].rearrange("p (b g r e) -> p b g r e", b=BATCH, g=WORD_CHUNKS, e=PAIR)
 
-            attention = []
-            for rows_sb in keys_sb[b]:
-                key_words = rows_sb[:].bitcast(F32).rearrange("p (j w) -> p j w", j=KEY_TILES)
-                kT = rotating.tile([P, WORD_CHUNKS * PAIR * BANK], BF16, tag="kT")
-                for g in range(WORD_CHUNKS):
-                    k_bank = psum.tile([P, BANK], F32, tag="bank")
-                    for j in range(KEY_TILES):
-                        transpose_words(
-                            k_bank[:, j * P : (j + 1) * P], key_words[:, j, g * P : (g + 1) * P]
-                        )
-                    piece = kT[:, g * PAIR * BANK : (g + 1) * PAIR * BANK]
-                    if g % 2 == 0:
-                        nc.scalar.copy(out=piece, in_=k_bank[:].bitcast(BF16))
-                    else:
-                        nc.vector.tensor_copy(out=piece, in_=k_bank[:].bitcast(BF16))
-                kT_view = kT[:].rearrange("p (g n e) -> p g n e", g=WORD_CHUNKS, e=PAIR)
+        def key_unit(rows_sb):
+            words = rows_sb[:].bitcast(F32).rearrange("p (j w) -> p j w", j=KEY_TILES)
+            kT = rotating.tile([P, WORD_CHUNKS * PAIR * BANK], BF16, tag="kT")
 
-                score = psum.tile([P, KEYS], F32, tag="bank")
-                for g in range(WORD_CHUNKS):
-                    for e in range(PAIR):
-                        nc.tensor.matmul(
-                            score[:],
-                            lhsT=qT_view[:, g, :, e],
-                            rhs=kT_view[:, g, :, e],
-                            start=(g == 0 and e == 0),
-                            stop=(g == WORD_CHUNKS - 1 and e == PAIR - 1),
-                        )
+            def transposes(bank, g, quarters):
+                for j in quarters:
+                    transpose_words(bank[:, j * P : (j + 1) * P], words[:, j, g * P : (g + 1) * P])
 
-                top = small.tile([P, 1], F32, tag="top")
-                nc.vector.reduce_max(out=top[:], in_=score[:], axis=AXIS.X)
-                shift = small.tile([P, 1], F32, tag="shift")
-                nc.vector.tensor_scalar_mul(out=shift[:], in0=top[:], scalar1=-SCALE)
-                attn = rotating.tile([P, KEYS], F32, tag="attn", bufs=4)
-                total = small.tile([P, 1], F32, tag="total")
-                nc.scalar.activation(
-                    out=attn[:],
-                    in_=score[:],
-                    func=ACT.Exp,
-                    bias=shift[:],
-                    scale=SCALE,
-                    accum_out=total[:],
-                )
-                inverse = small.tile([P, 1], F32, tag="inverse")
-                nc.vector.reciprocal(out=inverse[:], in_=total[:])
-                nc.vector.tensor_scalar_mul(out=attn[:], in0=attn[:], scalar1=inverse[:])
-                attention.append(attn)
+            def empty(bank, g):
+                piece = kT[:, g * PAIR * BANK : (g + 1) * PAIR * BANK]
+                if g < SHARED_VECTOR_BANKS:
+                    nc.vector.tensor_copy(out=piece, in_=bank[:].bitcast(BF16))
+                else:
+                    nc.scalar.copy(out=piece, in_=bank[:].bitcast(BF16))
 
+            view = kT[:].rearrange("p (g n e) -> p g n e", g=WORD_CHUNKS, e=PAIR)
+            return {"transposes": transposes, "empty": empty, "view": view}
+
+        def token_unit(rows_sb, vector_banks):
+            words = rows_sb[:].bitcast(F32).rearrange("p (j w) -> p j w", j=KEY_TILES)
+            grouped = rotating.tile([P, PASSES * KEYS * PACK], BF16, tag="x_grouped", align_bytes=64)
+            grouped_words = grouped[:].bitcast(F32).rearrange("p (g n u) -> p g n u", g=PASSES, u=2)
+            codes = rotating.tile([P, PASSES * KEYS], U32, tag="x_codes", align_bytes=64)
+            scales = rotating.tile([P, PASSES * KEYS], U8, tag="x_scales", align_bytes=64)
+
+            def transposes(bank, n, quarters):
+                g, half = divmod(n, 2)
+                for i in quarters:
+                    u, tile_in_half = divmod(i, 2)
+                    first = (2 * g + u) * P
+                    transpose_words(
+                        bank[:, i * P : (i + 1) * P],
+                        words[:, 2 * half + tile_in_half, first : first + P],
+                    )
+
+            def empty(bank, n):
+                g, half = divmod(n, 2)
+                piece = grouped_words[:, g, half * 2 * P : (half + 1) * 2 * P, :]
+                planes = bank[:].rearrange("p (u n) -> p n u", u=2)
+                if n < vector_banks:
+                    nc.vector.tensor_copy(out=piece, in_=planes)
+                else:
+                    nc.scalar.copy(out=piece, in_=planes)
+
+            def quantise():
+                for g in range(PASSES):
+                    nc.vector.quantize_mx(
+                        out=codes[:, g * KEYS : (g + 1) * KEYS].bitcast(FP8X4),
+                        scales=scales[:, g * KEYS : (g + 1) * KEYS],
+                        in_=grouped[:, g * KEYS * PACK : (g + 1) * KEYS * PACK],
+                    )
+
+            return {
+                "transposes": transposes,
+                "empty": empty,
+                "quantise": quantise,
+                "codes": codes,
+                "scales": scales,
+            }
+
+        def transpose_all(unit):
+            for n in range(UNIT_BANKS):
+                bank = psum.tile([P, BANK], F32, tag="bank")
+                unit["transposes"](bank, n, range(4))
+                unit["empty"](bank, n)
+
+        def softmax_start(score):
+            top = small.tile([P, 1], F32, tag="top")
+            nc.vector.reduce_max(out=top[:], in_=score[:], axis=AXIS.X)
+            shift = small.tile([P, 1], F32, tag="shift")
+            nc.vector.tensor_scalar_mul(out=shift[:], in0=top[:], scalar1=-SCALE)
+            attn = rotating.tile([P, KEYS], F32, tag="attn", bufs=4)
+            total = small.tile([P, 1], F32, tag="total")
+            nc.scalar.activation(
+                out=attn[:], in_=score[:], func=ACT.Exp, bias=shift[:], scale=SCALE, accum_out=total[:]
+            )
+            return attn, total
+
+        def softmax_finish(attn, total):
+            inverse = small.tile([P, 1], F32, tag="inverse")
+            nc.vector.reciprocal(out=inverse[:], in_=total[:])
+            nc.vector.tensor_scalar_mul(out=attn[:], in0=attn[:], scalar1=inverse[:])
+
+        def cast_votes(aw, awi):
             not_less = rotating.tile([P, KEYS], BF16, tag="not_less")
-            nc.vector.tensor_tensor(
-                out=not_less[:], in0=attention[0][:], in1=attention[1][:], op=ALU.is_ge
-            )
+            nc.vector.tensor_tensor(out=not_less[:], in0=aw[:], in1=awi[:], op=ALU.is_ge)
             not_more = rotating.tile([P, KEYS], BF16, tag="not_more")
-            nc.vector.tensor_tensor(
-                out=not_more[:], in0=attention[0][:], in1=attention[1][:], op=ALU.is_le
-            )
+            nc.vector.tensor_tensor(out=not_more[:], in0=aw[:], in1=awi[:], op=ALU.is_le)
+            return not_less, not_more
 
+        def count_votes(b, both_votes):
             counts = psum.tile([P, KEY_TILES * 2 * COUNT_COLS], F32, tag="bank")
             for j in range(KEY_TILES):
-                for side, votes in enumerate((not_less, not_more)):
+                for side, votes in enumerate(both_votes):
                     first = (2 * j + side) * COUNT_COLS
                     nc.tensor.matmul(
                         counts[:, first : first + COUNT_COLS],
@@ -162,62 +222,9 @@ def tile_crossattention_for_fusion_temporal_pa_kernel(tc, q, k, ki, xs, xis, Wv,
             )
             return factors
 
-        w_grouped = resident.tile([P, PASSES * DV * PACK], BF16, name="w_grouped", align_bytes=64)
-        w_codes = resident.tile([P, PASSES * DV], U32, name="w_codes", align_bytes=64)
-        w_scales = resident.tile([P, PASSES * DV], U8, name="w_scales", align_bytes=64)
-
-        def quantise_weights():
-            raw_view = w_raw[:].rearrange("p (g t d) -> p g t d", g=PASSES, t=PACK)
-            grouped_view = w_grouped[:].rearrange("p (g d t) -> p g d t", g=PASSES, t=PACK)
-            for h in range(DV_HALVES):
-                cols = slice(h * BANK, (h + 1) * BANK)
-                for g in range(PASSES):
-                    nc.vector.tensor_copy(
-                        out=grouped_view[:, g, cols, :].rearrange("p (c i) t -> p c t i", i=4),
-                        in_=raw_view[:, g, :, cols].rearrange("p t (c i) -> p c t i", i=4),
-                    )
-                for g in range(PASSES):
-                    first = g * DV + h * BANK
-                    nc.vector.quantize_mx(
-                        out=w_codes[:, first : first + BANK].bitcast(FP8X4),
-                        scales=w_scales[:, first : first + BANK],
-                        in_=w_grouped[:, PACK * first : PACK * (first + BANK)],
-                    )
-
-        def quantise_tokens(rows_sb):
-            x_words = rows_sb[:].bitcast(F32).rearrange("p (j w) -> p j w", j=KEY_TILES)
-            grouped = rotating.tile([P, PASSES * KEYS * PACK], BF16, tag="x_grouped", align_bytes=64)
-            grouped_words = grouped[:].bitcast(F32).rearrange("p (g n u) -> p g n u", g=PASSES, u=2)
-            codes = rotating.tile([P, PASSES * KEYS], U32, tag="x_codes", align_bytes=64)
-            scales = rotating.tile([P, PASSES * KEYS], U8, tag="x_scales", align_bytes=64)
-            for g in range(PASSES):
-                for half in range(KEY_TILES // 2):
-                    x_bank = psum.tile([P, BANK], F32, tag="bank")
-                    bank_view = x_bank[:].rearrange("p (u n) -> p u n", u=2)
-                    for u in range(2):
-                        for i in range(2):
-                            first_word = (2 * g + u) * P
-                            transpose_words(
-                                bank_view[:, u, i * P : (i + 1) * P],
-                                x_words[:, 2 * half + i, first_word : first_word + P],
-                            )
-                    nc.scalar.copy(
-                        out=grouped_words[:, g, half * 2 * P : (half + 1) * 2 * P, :],
-                        in_=x_bank[:].rearrange("p (u n) -> p n u", u=2),
-                    )
-            for g in range(PASSES):
-                nc.vector.quantize_mx(
-                    out=codes[:, g * KEYS : (g + 1) * KEYS].bitcast(FP8X4),
-                    scales=scales[:, g * KEYS : (g + 1) * KEYS],
-                    in_=grouped[:, g * KEYS * PACK : (g + 1) * KEYS * PACK],
-                )
-            return codes, scales
-
-        def project(b, stream, codes, scales, factors, scaled_v):
+        def project(b, stream, unit, factors, scaled_v, key_tiles):
             out_view = out[b].rearrange("(p j) d -> p j d", j=KEY_TILES)
-            for j in range(KEY_TILES):
-                if stream == 1:
-                    mixed = rotating.tile([P, DV], F32, tag="mixed", bufs=3)
+            for j in key_tiles:
                 for h in range(DV_HALVES):
                     acc = psum.tile([P, BANK], F32, tag="bank")
                     for g in range(PASSES):
@@ -225,8 +232,8 @@ def tile_crossattention_for_fusion_temporal_pa_kernel(tc, q, k, ki, xs, xis, Wv,
                         cols = slice(g * DV + h * BANK, g * DV + (h + 1) * BANK)
                         nc.tensor.matmul_mx(
                             out=acc[:],
-                            lhsT=codes[:, tokens].bitcast(FP8X4),
-                            lhsT_scale=scales[:, tokens],
+                            lhsT=unit["codes"][:, tokens].bitcast(FP8X4),
+                            lhsT_scale=unit["scales"][:, tokens],
                             rhs=w_codes[:, cols].bitcast(FP8X4),
                             rhs_scale=w_scales[:, cols],
                             start=(g == 0),
@@ -238,27 +245,70 @@ def tile_crossattention_for_fusion_temporal_pa_kernel(tc, q, k, ki, xs, xis, Wv,
                             out=kept, in_=acc[:], func=ACT.Copy, scale=factors[:, 2 * j : 2 * j + 1]
                         )
                     else:
+                        mixed = rotating.tile([P, BANK], F32, tag="mixed", bufs=4)
                         nc.vector.scalar_tensor_tensor(
-                            out=mixed[:, h * BANK : (h + 1) * BANK],
+                            out=mixed[:],
                             in0=acc[:],
                             scalar=factors[:, 2 * j + 1 : 2 * j + 2],
                             in1=kept,
                             op0=ALU.mult,
                             op1=ALU.add,
                         )
-                if stream == 1:
-                    nc.sync.dma_start(out=out_view[:, j, :], in_=mixed[:])
+                        nc.sync.dma_start(
+                            out=out_view[:, j, h * BANK : (h + 1) * BANK], in_=mixed[:]
+                        )
 
-        factors_of = [None] * BATCH
-        factors_of[0] = mix_factors(0)
-        quantise_weights()
-        factors_of[1] = mix_factors(1)
-        ready = quantise_tokens(tokens_sb[0])
-        for b in range(BATCH):
-            scaled_v = rotating.tile([P, KEY_TILES * DV], F32, tag="scaled_v")
-            for stream in range(2):
-                codes, scales = ready
-                following = 2 * b + stream + 1
-                if following < len(tokens_sb):
-                    ready = quantise_tokens(tokens_sb[following])
-                project(b, stream, codes, scales, factors_of[b], scaled_v)
+        following = key_unit(keys_sb[0])
+        transpose_all(following)
+        scores = []
+        softmaxes = []
+        votes_of = []
+        for s in range(len(keys_sb)):
+            current = following
+            if s + 1 < len(keys_sb):
+                following = key_unit(keys_sb[s + 1])
+            else:
+                following = token_unit(tokens_sb[0], SHARED_VECTOR_BANKS)
+            if s >= 1:
+                softmaxes.append(softmax_start(scores[s - 1]))
+            score = psum.tile([P, KEYS], F32, tag="bank")
+            scores.append(score)
+            for g in range(WORD_CHUNKS):
+                bank = psum.tile([P, BANK], F32, tag="bank")
+                for e in range(PAIR):
+                    following["transposes"](bank, g, range(2 * e, 2 * e + 2))
+                    nc.tensor.matmul(
+                        score[:],
+                        lhsT=qT_view[:, s // 2, g, :, e],
+                        rhs=current["view"][:, g, :, e],
+                        start=(g == 0 and e == 0),
+                        stop=(g == WORD_CHUNKS - 1 and e == PAIR - 1),
+                    )
+                following["empty"](bank, g)
+            if s >= 1:
+                softmax_finish(*softmaxes[s - 1])
+            if s == 2:
+                votes_of.append(cast_votes(softmaxes[0][0], softmaxes[1][0]))
+
+        units = [following]
+        units[0]["quantise"]()
+        factors_of = [count_votes(0, votes_of[0])]
+        softmaxes.append(softmax_start(scores[3]))
+        units.append(token_unit(tokens_sb[1], UNIT_BANKS))
+        transpose_all(units[1])
+        softmax_finish(*softmaxes[3])
+        votes_of.append(cast_votes(softmaxes[2][0], softmaxes[3][0]))
+
+        for i in range(len(tokens_sb)):
+            b, stream = divmod(i, 2)
+            if stream == 0:
+                scaled_v = rotating.tile([P, KEY_TILES * DV], F32, tag="scaled_v")
+            project(b, stream, units[i], factors_of[b], scaled_v, range(0, KEY_TILES // 2))
+            if i + 1 < len(tokens_sb):
+                units[i + 1]["quantise"]()
+            project(b, stream, units[i], factors_of[b], scaled_v, range(KEY_TILES // 2, KEY_TILES))
+            if i == 0:
+                factors_of.append(count_votes(1, votes_of[1]))
+            if i + 2 < len(tokens_sb):
+                units.append(token_unit(tokens_sb[i + 2], UNIT_BANKS * (i % 2)))
+                transpose_all(units[i + 2])

@@ -27,7 +27,6 @@ BANK = 512
 DV_HALVES = DV // BANK
 COUNT_COLS = 32
 UNIT_BANKS = 4
-SHARED_VECTOR_BANKS = 1
 SCALE = C**-0.5
 
 FLOPS = 2 * BATCH * 2 * QUERIES * KEYS * C + 2 * BATCH * 2 * KEYS * C * DV
@@ -39,16 +38,8 @@ def tile_crossattention_for_fusion_temporal_pa_kernel(tc, q, k, ki, xs, xis, Wv,
         resident = ctx.enter_context(tc.tile_pool(name="resident", bufs=1))
         rotating = ctx.enter_context(tc.tile_pool(name="rotating", bufs=2))
         small = ctx.enter_context(tc.tile_pool(name="small", bufs=4))
-        psum = ctx.enter_context(tc.psum_pool(name="psum", bufs=8))
+        psum = ctx.enter_context(tc.psum_pool(name="psum", bufs=6))
         ctx.enter_context(tc.manual_schedule())
-
-        w_raw = resident.tile([P, PASSES * PACK * DV], BF16, name="w_raw")
-        halves_view = w_raw[:].rearrange("p (g u e d) -> p g u e d", g=PASSES, u=2, e=PAIR)
-        for g in range(PASSES):
-            rows = Wv[g * P * PACK : (g + 1) * P * PACK, :]
-            nc.sync.dma_start(
-                out=halves_view[:, g], in_=rows.rearrange("(u p e) d -> p u e d", u=2, e=PAIR)
-            )
 
         q_sb = resident.tile([P, BATCH * C], BF16, name="q_sb")
         nc.sync.dma_start(
@@ -60,11 +51,20 @@ def tile_crossattention_for_fusion_temporal_pa_kernel(tc, q, k, ki, xs, xis, Wv,
             nc.sync.dma_start(out=rows_sb[:], in_=rows.rearrange("(p j) c -> p (j c)", j=KEY_TILES))
             return rows_sb
 
-        keys_sb = [
-            load_rows("keys_sb%d%d" % (b, stream), rows[b])
-            for b in range(BATCH)
-            for stream, rows in enumerate((k, ki))
-        ]
+        w_raw = resident.tile([P, PASSES * PACK * DV], BF16, name="w_raw")
+        halves_view = w_raw[:].rearrange("p (g u e d) -> p g u e d", g=PASSES, u=2, e=PAIR)
+
+        def load_weights(g):
+            rows = Wv[g * P * PACK : (g + 1) * P * PACK, :]
+            nc.sync.dma_start(
+                out=halves_view[:, g], in_=rows.rearrange("(u p e) d -> p u e d", u=2, e=PAIR)
+            )
+
+        keys_sb = [load_rows("keys_sb00", k[0]), load_rows("keys_sb01", ki[0])]
+        load_weights(0)
+        keys_sb.append(load_rows("keys_sb10", k[1]))
+        load_weights(1)
+        keys_sb.append(load_rows("keys_sb11", ki[1]))
         tokens_sb = [
             load_rows("tokens_sb%d%d" % (b, stream), rows[b])
             for b in range(BATCH)
@@ -85,14 +85,16 @@ def tile_crossattention_for_fusion_temporal_pa_kernel(tc, q, k, ki, xs, xis, Wv,
         w_scales = resident.tile([P, PASSES * DV], U8, name="w_scales", align_bytes=64)
         raw_view = w_raw[:].rearrange("p (g t d) -> p g t d", g=PASSES, t=PACK)
         grouped_view = w_grouped[:].rearrange("p (g d t) -> p g d t", g=PASSES, t=PACK)
-        for g in range(PASSES):
+
+        def regroup_weights(g):
             for h in range(DV_HALVES):
                 cols = slice(h * BANK, (h + 1) * BANK)
                 nc.vector.tensor_copy(
                     out=grouped_view[:, g, cols, :].rearrange("p (c i) t -> p c t i", i=4),
                     in_=raw_view[:, g, :, cols].rearrange("p t (c i) -> p c t i", i=4),
                 )
-        for g in range(PASSES):
+
+        def quantise_weights(g):
             nc.vector.quantize_mx(
                 out=w_codes[:, g * DV : (g + 1) * DV].bitcast(FP8X4),
                 scales=w_scales[:, g * DV : (g + 1) * DV],
@@ -124,15 +126,12 @@ def tile_crossattention_for_fusion_temporal_pa_kernel(tc, q, k, ki, xs, xis, Wv,
 
             def empty(bank, g):
                 piece = kT[:, g * PAIR * BANK : (g + 1) * PAIR * BANK]
-                if g < SHARED_VECTOR_BANKS:
-                    nc.vector.tensor_copy(out=piece, in_=bank[:].bitcast(BF16))
-                else:
-                    nc.scalar.copy(out=piece, in_=bank[:].bitcast(BF16))
+                nc.scalar.copy(out=piece, in_=bank[:].bitcast(BF16))
 
             view = kT[:].rearrange("p (g n e) -> p g n e", g=WORD_CHUNKS, e=PAIR)
             return {"transposes": transposes, "empty": empty, "view": view}
 
-        def token_unit(rows_sb, vector_banks):
+        def token_unit(rows_sb, copy_out):
             words = rows_sb[:].bitcast(F32).rearrange("p (j w) -> p j w", j=KEY_TILES)
             grouped = rotating.tile([P, PASSES * KEYS * PACK], BF16, tag="x_grouped", align_bytes=64)
             grouped_words = grouped[:].bitcast(F32).rearrange("p (g n u) -> p g n u", g=PASSES, u=2)
@@ -151,20 +150,17 @@ def tile_crossattention_for_fusion_temporal_pa_kernel(tc, q, k, ki, xs, xis, Wv,
 
             def empty(bank, n):
                 g, half = divmod(n, 2)
-                piece = grouped_words[:, g, half * 2 * P : (half + 1) * 2 * P, :]
-                planes = bank[:].rearrange("p (u n) -> p n u", u=2)
-                if n < vector_banks:
-                    nc.vector.tensor_copy(out=piece, in_=planes)
-                else:
-                    nc.scalar.copy(out=piece, in_=planes)
+                copy_out(
+                    out=grouped_words[:, g, half * 2 * P : (half + 1) * 2 * P, :],
+                    in_=bank[:].rearrange("p (u n) -> p n u", u=2),
+                )
 
-            def quantise():
-                for g in range(PASSES):
-                    nc.vector.quantize_mx(
-                        out=codes[:, g * KEYS : (g + 1) * KEYS].bitcast(FP8X4),
-                        scales=scales[:, g * KEYS : (g + 1) * KEYS],
-                        in_=grouped[:, g * KEYS * PACK : (g + 1) * KEYS * PACK],
-                    )
+            def quantise(g):
+                nc.vector.quantize_mx(
+                    out=codes[:, g * KEYS : (g + 1) * KEYS].bitcast(FP8X4),
+                    scales=scales[:, g * KEYS : (g + 1) * KEYS],
+                    in_=grouped[:, g * KEYS * PACK : (g + 1) * KEYS * PACK],
+                )
 
             return {
                 "transposes": transposes,
@@ -180,11 +176,14 @@ def tile_crossattention_for_fusion_temporal_pa_kernel(tc, q, k, ki, xs, xis, Wv,
                 unit["transposes"](bank, n, range(4))
                 unit["empty"](bank, n)
 
-        def softmax_start(score):
+        def softmax_shift(score):
             top = small.tile([P, 1], F32, tag="top")
             nc.vector.reduce_max(out=top[:], in_=score[:], axis=AXIS.X)
             shift = small.tile([P, 1], F32, tag="shift")
             nc.vector.tensor_scalar_mul(out=shift[:], in0=top[:], scalar1=-SCALE)
+            return shift
+
+        def softmax_exp(score, shift):
             attn = rotating.tile([P, KEYS], F32, tag="attn", bufs=4)
             total = small.tile([P, 1], F32, tag="total")
             nc.scalar.activation(
@@ -205,7 +204,7 @@ def tile_crossattention_for_fusion_temporal_pa_kernel(tc, q, k, ki, xs, xis, Wv,
             return not_less, not_more
 
         def count_votes(b, both_votes):
-            counts = psum.tile([P, KEY_TILES * 2 * COUNT_COLS], F32, tag="bank")
+            counts = psum.tile([P, KEY_TILES * 2 * COUNT_COLS], F32, tag="score", bufs=2)
             for j in range(KEY_TILES):
                 for side, votes in enumerate(both_votes):
                     first = (2 * j + side) * COUNT_COLS
@@ -258,46 +257,50 @@ def tile_crossattention_for_fusion_temporal_pa_kernel(tc, q, k, ki, xs, xis, Wv,
                             out=out_view[:, j, h * BANK : (h + 1) * BANK], in_=mixed[:]
                         )
 
-        following = key_unit(keys_sb[0])
-        transpose_all(following)
+        copy_out_of = (nc.scalar.copy, nc.vector.tensor_copy)
+        weight_steps = (regroup_weights, regroup_weights, quantise_weights, quantise_weights)
+        line = [key_unit(keys_sb[0])]
+        transpose_all(line[0])
         scores = []
         softmaxes = []
-        votes_of = []
         for s in range(len(keys_sb)):
-            current = following
             if s + 1 < len(keys_sb):
-                following = key_unit(keys_sb[s + 1])
+                line.append(key_unit(keys_sb[s + 1]))
             else:
-                following = token_unit(tokens_sb[0], SHARED_VECTOR_BANKS)
+                line.append(token_unit(tokens_sb[0], copy_out_of[0]))
             if s >= 1:
-                softmaxes.append(softmax_start(scores[s - 1]))
-            score = psum.tile([P, KEYS], F32, tag="bank")
+                shift = softmax_shift(scores[s - 1])
+            weight_steps[s](s % PASSES)
+            score = psum.tile([P, KEYS], F32, tag="score", bufs=2)
             scores.append(score)
             for g in range(WORD_CHUNKS):
                 bank = psum.tile([P, BANK], F32, tag="bank")
                 for e in range(PAIR):
-                    following["transposes"](bank, g, range(2 * e, 2 * e + 2))
+                    line[s + 1]["transposes"](bank, g, range(2 * e, 2 * e + 2))
                     nc.tensor.matmul(
                         score[:],
                         lhsT=qT_view[:, s // 2, g, :, e],
-                        rhs=current["view"][:, g, :, e],
+                        rhs=line[s]["view"][:, g, :, e],
                         start=(g == 0 and e == 0),
                         stop=(g == WORD_CHUNKS - 1 and e == PAIR - 1),
                     )
-                following["empty"](bank, g)
+                line[s + 1]["empty"](bank, g)
+                if g == 0 and s >= 1:
+                    softmaxes.append(softmax_exp(scores[s - 1], shift))
             if s >= 1:
                 softmax_finish(*softmaxes[s - 1])
             if s == 2:
-                votes_of.append(cast_votes(softmaxes[0][0], softmaxes[1][0]))
+                votes_0 = cast_votes(softmaxes[0][0], softmaxes[1][0])
 
-        units = [following]
-        units[0]["quantise"]()
-        factors_of = [count_votes(0, votes_of[0])]
-        softmaxes.append(softmax_start(scores[3]))
-        units.append(token_unit(tokens_sb[1], UNIT_BANKS))
+        units = [line[len(keys_sb)], token_unit(tokens_sb[1], copy_out_of[1])]
+        units[0]["quantise"](0)
+        shift = softmax_shift(scores[3])
+        softmaxes.append(softmax_exp(scores[3], shift))
+        units[0]["quantise"](1)
+        factors_of = [count_votes(0, votes_0)]
         transpose_all(units[1])
         softmax_finish(*softmaxes[3])
-        votes_of.append(cast_votes(softmaxes[2][0], softmaxes[3][0]))
+        votes_1 = cast_votes(softmaxes[2][0], softmaxes[3][0])
 
         for i in range(len(tokens_sb)):
             b, stream = divmod(i, 2)
@@ -305,10 +308,11 @@ def tile_crossattention_for_fusion_temporal_pa_kernel(tc, q, k, ki, xs, xis, Wv,
                 scaled_v = rotating.tile([P, KEY_TILES * DV], F32, tag="scaled_v")
             project(b, stream, units[i], factors_of[b], scaled_v, range(0, KEY_TILES // 2))
             if i + 1 < len(tokens_sb):
-                units[i + 1]["quantise"]()
+                for g in range(PASSES):
+                    units[i + 1]["quantise"](g)
             project(b, stream, units[i], factors_of[b], scaled_v, range(KEY_TILES // 2, KEY_TILES))
-            if i == 0:
-                factors_of.append(count_votes(1, votes_of[1]))
+            if i + 1 == 2:
+                factors_of.append(count_votes(1, votes_1))
             if i + 2 < len(tokens_sb):
-                units.append(token_unit(tokens_sb[i + 2], UNIT_BANKS * (i % 2)))
+                units.append(token_unit(tokens_sb[i + 2], copy_out_of[stream]))
                 transpose_all(units[i + 2])

@@ -112,7 +112,7 @@ def tile_crossattention_for_fusion_temporal_pa_kernel(tc, q, k, ki, xs, xis, Wv,
                 first = (b * WORD_CHUNKS + g) * P
                 transpose_words(q_bank[:, g * P : (g + 1) * P], q_words[:, first : first + P])
             nc.scalar.copy(
-                out=qT[:, b * PAIR * BANK : (b + 1) * PAIR * BANK], in_=q_bank[:].bitcast(BF16)
+                out=qT[:, b * PAIR * BANK : (b + 1) * PAIR * BANK].bitcast(F32), in_=q_bank[:]
             )
         qT_view = qT[:].rearrange("p (b g r e) -> p b g r e", b=BATCH, g=WORD_CHUNKS, e=PAIR)
 
@@ -126,7 +126,7 @@ def tile_crossattention_for_fusion_temporal_pa_kernel(tc, q, k, ki, xs, xis, Wv,
 
             def empty(bank, g):
                 piece = kT[:, g * PAIR * BANK : (g + 1) * PAIR * BANK]
-                nc.scalar.copy(out=piece, in_=bank[:].bitcast(BF16))
+                nc.scalar.copy(out=piece.bitcast(F32), in_=bank[:])
 
             view = kT[:].rearrange("p (g n e) -> p g n e", g=WORD_CHUNKS, e=PAIR)
             return {"transposes": transposes, "empty": empty, "view": view}

from contextlib import ExitStack

import concourse.mybir as mybir
from concourse.masks import make_identity

BF16 = mybir.dt.bfloat16
F32 = mybir.dt.float32
U32 = mybir.dt.uint32
U8 = mybir.dt.uint8
FP8X4 = mybir.dt.float8_e4m3fn_x4
ALU = mybir.AluOpType
ACT = mybir.ActivationFunctionType
AXIS = mybir.AxisListType

P = 128
BATCH = 2
QUERIES = 128
KEYS = 512
C = 1024
DV = 1024
KEY_TILES = KEYS // P
PAIR = 2
WORD_CHUNKS = C // PAIR // P
PACK = 4
PASSES = C // (P * PACK)
BANK = 512
DV_HALVES = DV // BANK
COUNT_COLS = 32
UNIT_BANKS = 4
SCALE = C**-0.5

FLOPS = 2 * BATCH * 2 * QUERIES * KEYS * C + 2 * BATCH * 2 * KEYS * C * DV


def tile_crossattention_for_fusion_temporal_pa_kernel(tc, q, k, ki, xs, xis, Wv, out):
    nc = tc.nc
    with ExitStack() as ctx:
        resident = ctx.enter_context(tc.tile_pool(name="resident", bufs=1))
        rotating = ctx.enter_context(tc.tile_pool(name="rotating", bufs=2))
        small = ctx.enter_context(tc.tile_pool(name="small", bufs=4))
        psum = ctx.enter_context(tc.psum_pool(name="psum", bufs=6))
        ctx.enter_context(tc.manual_schedule())

        q_sb = resident.tile([P, BATCH * C], BF16, name="q_sb")
        nc.sync.dma_start(
            out=q_sb[:].rearrange("p (b c) -> p b c", b=BATCH), in_=q.rearrange("b r c -> r b c")
        )

        def load_rows(name, rows):
            rows_sb = resident.tile([P, KEY_TILES * C], BF16, name=name)
            nc.sync.dma_start(out=rows_sb[:], in_=rows.rearrange("(p j) c -> p (j c)", j=KEY_TILES))
            return rows_sb

        w_raw = resident.tile([P, PASSES * PACK * DV], BF16, name="w_raw")
        halves_view = w_raw[:].rearrange("p (g u e d) -> p g u e d", g=PASSES, u=2, e=PAIR)

        def load_weights(g):
            rows = Wv[g * P * PACK : (g + 1) * P * PACK, :]
            nc.sync.dma_start(
                out=halves_view[:, g], in_=rows.rearrange("(u p e) d -> p u e d", u=2, e=PAIR)
            )

        keys_sb = [load_rows("keys_sb00", k[0]), load_rows("keys_sb01", ki[0])]
        load_weights(0)
        keys_sb.append(load_rows("keys_sb10", k[1]))
        load_weights(1)
        keys_sb.append(load_rows("keys_sb11", ki[1]))
        tokens_sb = [
            load_rows("tokens_sb%d%d" % (b, stream), rows[b])
            for b in range(BATCH)
            for stream, rows in enumerate((xs, xis))
        ]

        ident = resident.tile([P, P], F32, name="ident")
        make_identity(nc, ident[:])
        vote_share = resident.tile([P, COUNT_COLS], BF16, name="vote_share")
        nc.vector.memset(vote_share[:], 1.0 / QUERIES)
        zero = small.tile([P, 1], F32, tag="zero")
        nc.vector.memset(zero[:], 0.0)
        one = small.tile([P, 1], F32, tag="one")
        nc.scalar.activation(out=one[:], in_=zero[:], func=ACT.Exp)

        w_grouped = resident.tile([P, PASSES * DV * PACK], BF16, name="w_grouped", align_bytes=64)
        w_codes = resident.tile([P, PASSES * DV], U32, name="w_codes", align_bytes=64)
        w_scales = resident.tile([P, PASSES * DV], U8, name="w_scales", align_bytes=64)
        raw_view = w_raw[:].rearrange("p (g t d) -> p g t d", g=PASSES, t=PACK)
        grouped_view = w_grouped[:].rearrange("p (g d t) -> p g d t", g=PASSES, t=PACK)

        def regroup_weights(g):
            for h in range(DV_HALVES):
                cols = slice(h * BANK, (h + 1) * BANK)
                nc.vector.tensor_copy(
                    out=grouped_view[:, g, cols, :].rearrange("p (c i) t -> p c t i", i=4),
                    in_=raw_view[:, g, :, cols].rearrange("p t (c i) -> p c t i", i=4),
                )

        def quantise_weights(g):
            nc.vector.quantize_mx(
                out=w_codes[:, g * DV : (g + 1) * DV].bitcast(FP8X4),
                scales=w_scales[:, g * DV : (g + 1) * DV],
                in_=w_grouped[:, g * DV * PACK : (g + 1) * DV * PACK],
            )

        def transpose_words(bank_cols, words):
            nc.tensor.transpose(bank_cols, words, ident[:])

        qT = resident.tile([P, BATCH * PAIR * BANK], BF16, name="qT")
        q_words = q_sb[:].bitcast(F32)
        for b in range(BATCH):
            q_bank = psum.tile([P, BANK], F32, tag="bank")
            for g in range(WORD_CHUNKS):
                first = (b * WORD_CHUNKS + g) * P
                transpose_words(q_bank[:, g * P : (g + 1) * P], q_words[:, first : first + P])
            nc.scalar.copy(
                out=qT[:, b * PAIR * BANK : (b + 1) * PAIR * BANK].bitcast(F32), in_=q_bank[:]
            )
        qT_view = qT[:].rearrange("p (b g r e) -> p b g r e", b=BATCH, g=WORD_CHUNKS, e=PAIR)

        def key_unit(rows_sb):
            words = rows_sb[:].bitcast(F32).rearrange("p (j w) -> p j w", j=KEY_TILES)
            kT = rotating.tile([P, WORD_CHUNKS * PAIR * BANK], BF16, tag="kT")

            def transposes(bank, g, quarters):
                for j in quarters:
                    transpose_words(bank[:, j * P : (j + 1) * P], words[:, j, g * P : (g + 1) * P])

            def empty(bank, g):
                piece = kT[:, g * PAIR * BANK : (g + 1) * PAIR * BANK]
                nc.scalar.copy(out=piece.bitcast(F32), in_=bank[:])

            view = kT[:].rearrange("p (g n e) -> p g n e", g=WORD_CHUNKS, e=PAIR)
            return {"transposes": transposes, "empty": empty, "view": view}

        def token_unit(rows_sb, copy_out):
            words = rows_sb[:].bitcast(F32).rearrange("p (j w) -> p j w", j=KEY_TILES)
            grouped = rotating.tile([P, PASSES * KEYS * PACK], BF16, tag="x_grouped", align_bytes=64)
            grouped_words = grouped[:].bitcast(F32).rearrange("p (g n u) -> p g n u", g=PASSES, u=2)
            codes = rotating.tile([P, PASSES * KEYS], U32, tag="x_codes", align_bytes=64)
            scales = rotating.tile([P, PASSES * KEYS], U8, tag="x_scales", align_bytes=64)

            def transposes(bank, n, quarters):
                g, half = divmod(n, 2)
                for i in quarters:
                    u, tile_in_half = divmod(i, 2)
                    first = (2 * g + u) * P
                    transpose_words(
                        bank[:, i * P : (i + 1) * P],
                        words[:, 2 * half + tile_in_half, first : first + P],
                    )

            def empty(bank, n):
                g, half = divmod(n, 2)
                copy_out(
                    out=grouped_words[:, g, half * 2 * P : (half + 1) * 2 * P, :],
                    in_=bank[:].rearrange("p (u n) -> p n u", u=2),
                )

            def quantise(g):
                nc.vector.quantize_mx(
                    out=codes[:, g * KEYS : (g + 1) * KEYS].bitcast(FP8X4),
                    scales=scales[:, g * KEYS : (g + 1) * KEYS],
                    in_=grouped[:, g * KEYS * PACK : (g + 1) * KEYS * PACK],
                )

            return {
                "transposes": transposes,
                "empty": empty,
                "quantise": quantise,
                "codes": codes,
                "scales": scales,
            }

        def transpose_all(unit):
            for n in range(UNIT_BANKS):
                bank = psum.tile([P, BANK], F32, tag="bank")
                unit["transposes"](bank, n, range(4))
                unit["empty"](bank, n)

        def softmax_shift(score):
            top = small.tile([P, 1], F32, tag="top")
            nc.vector.reduce_max(out=top[:], in_=score[:], axis=AXIS.X)
            shift = small.tile([P, 1], F32, tag="shift")
            nc.vector.tensor_scalar_mul(out=shift[:], in0=top[:], scalar1=-SCALE)
            return shift

        def softmax_exp(score, shift):
            attn = rotating.tile([P, KEYS], F32, tag="attn", bufs=4)
            total = small.tile([P, 1], F32, tag="total")
            nc.scalar.activation(
                out=attn[:], in_=score[:], func=ACT.Exp, bias=shift[:], scale=SCALE, accum_out=total[:]
            )
            return attn, total

        def softmax_finish(attn, total):
            inverse = small.tile([P, 1], F32, tag="inverse")
            nc.vector.reciprocal(out=inverse[:], in_=total[:])
            nc.vector.tensor_scalar_mul(out=attn[:], in0=attn[:], scalar1=inverse[:])

        def cast_votes(aw, awi):
            not_less = rotating.tile([P, KEYS], BF16, tag="not_less")
            nc.vector.tensor_tensor(out=not_less[:], in0=aw[:], in1=awi[:], op=ALU.is_ge)
            not_more = rotating.tile([P, KEYS], BF16, tag="not_more")
            nc.vector.tensor_tensor(out=not_more[:], in0=aw[:], in1=awi[:], op=ALU.is_le)
            return not_less, not_more

        def count_votes(b, both_votes):
            counts = psum.tile([P, KEY_TILES * 2 * COUNT_COLS], F32, tag="score", bufs=2)
            for j in range(KEY_TILES):
                for side, votes in enumerate(both_votes):
                    first = (2 * j + side) * COUNT_COLS
                    nc.tensor.matmul(
                        counts[:, first : first + COUNT_COLS],
                        lhsT=votes[:, j * P : (j + 1) * P],
                        rhs=vote_share[:],
                        start=True,
                        stop=True,
                    )
            factors = resident.tile([P, KEY_TILES * 2], F32, name="factors%d" % b)
            nc.vector.tensor_copy(
                out=factors[:], in_=counts[:].rearrange("p (i n) -> p i n", n=COUNT_COLS)[:, :, 0]
            )
            return factors

        def project(b, stream, unit, factors, scaled_v, key_tiles):
            out_view = out[b].rearrange("(p j) d -> p j d", j=KEY_TILES)
            for j in key_tiles:
                for h in range(DV_HALVES):
                    acc = psum.tile([P, BANK], F32, tag="bank")
                    for g in range(PASSES):
                        tokens = slice(g * KEYS + j * P, g * KEYS + (j + 1) * P)
                        cols = slice(g * DV + h * BANK, g * DV + (h + 1) * BANK)
                        nc.tensor.matmul_mx(
                            out=acc[:],
                            lhsT=unit["codes"][:, tokens].bitcast(FP8X4),
                            lhsT_scale=unit["scales"][:, tokens],
                            rhs=w_codes[:, cols].bitcast(FP8X4),
                            rhs_scale=w_scales[:, cols],
                            start=(g == 0),
                            stop=(g == PASSES - 1),
                        )
                    kept = scaled_v[:, j * DV + h * BANK : j * DV + (h + 1) * BANK]
                    if stream == 0:
                        nc.scalar.activation(
                            out=kept, in_=acc[:], func=ACT.Copy, scale=factors[:, 2 * j : 2 * j + 1]
                        )
                    else:
                        mixed = rotating.tile([P, BANK], F32, tag="mixed", bufs=4)
                        nc.vector.scalar_tensor_tensor(
                            out=mixed[:],
                            in0=acc[:],
                            scalar=factors[:, 2 * j + 1 : 2 * j + 2],
                            in1=kept,
                            op0=ALU.mult,
                            op1=ALU.add,
                        )
                        nc.sync.dma_start(
                            out=out_view[:, j, h * BANK : (h + 1) * BANK], in_=mixed[:]
                        )

        copy_out_of = (nc.scalar.copy, nc.vector.tensor_copy)
        weight_steps = (regroup_weights, regroup_weights, quantise_weights, quantise_weights)
        line = [key_unit(keys_sb[0])]
        transpose_all(line[0])
        scores = []
        softmaxes = []
        for s in range(len(keys_sb)):
            if s + 1 < len(keys_sb):
                line.append(key_unit(keys_sb[s + 1]))
            else:
                line.append(token_unit(tokens_sb[0], copy_out_of[0]))
            if s >= 1:
                shift = softmax_shift(scores[s - 1])
            weight_steps[s](s % PASSES)
            score = psum.tile([P, KEYS], F32, tag="score", bufs=2)
            scores.append(score)
            for g in range(WORD_CHUNKS):
                bank = psum.tile([P, BANK], F32, tag="bank")
                for e in range(PAIR):
                    line[s + 1]["transposes"](bank, g, range(2 * e, 2 * e + 2))
                    nc.tensor.matmul(
                        score[:],
                        lhsT=qT_view[:, s // 2, g, :, e],
                        rhs=line[s]["view"][:, g, :, e],
                        start=(g == 0 and e == 0),
                        stop=(g == WORD_CHUNKS - 1 and e == PAIR - 1),
                    )
                line[s + 1]["empty"](bank, g)
                if g == 0 and s >= 1:
                    softmaxes.append(softmax_exp(scores[s - 1], shift))
            if s >= 1:
                softmax_finish(*softmaxes[s - 1])
            if s == 2:
                votes_0 = cast_votes(softmaxes[0][0], softmaxes[1][0])

        units = [line[len(keys_sb)], token_unit(tokens_sb[1], copy_out_of[1])]
        units[0]["quantise"](0)
        shift = softmax_shift(scores[3])
        softmaxes.append(softmax_exp(scores[3], shift))
        units[0]["quantise"](1)
        factors_of = [count_votes(0, votes_0)]
        transpose_all(units[1])
        softmax_finish(*softmaxes[3])
        votes_1 = cast_votes(softmaxes[2][0], softmaxes[3][0])

        for i in range(len(tokens_sb)):
            b, stream = divmod(i, 2)
            if stream == 0:
                scaled_v = rotating.tile([P, KEY_TILES * DV], F32, tag="scaled_v")
            project(b, stream, units[i], factors_of[b], scaled_v, range(0, KEY_TILES // 2))
            if i + 1 < len(tokens_sb):
                for g in range(PASSES):
                    units[i + 1]["quantise"](g)
            project(b, stream, units[i], factors_of[b], scaled_v, range(KEY_TILES // 2, KEY_TILES))
            if i + 1 == 2:
                factors_of.append(count_votes(1, votes_1))
            if i + 2 < len(tokens_sb):
                units.append(token_unit(tokens_sb[i + 2], copy_out_of[stream]))
                transpose_all(units[i + 2])
